import numpy as np
import ml_dtypes


def mxq(x, axis, fmt="e4m3"):
    dtype, down = {"e4m3": (ml_dtypes.float8_e4m3fn, 7), "e5m2": (ml_dtypes.float8_e5m2, 14)}[fmt]
    v = np.moveaxis(np.asarray(x, np.float32).astype(ml_dtypes.bfloat16).astype(np.float64), axis, -1)
    blocks = v.reshape(v.shape[:-1] + (-1, 32))
    amax = np.abs(blocks).max(-1, keepdims=True)
    byte = np.maximum(np.where(amax > 0, np.frexp(amax)[1] - 1 + 127, 0) - down, 1)
    scale = np.exp2(byte - 127.0)
    codes = (blocks / scale).astype(np.float32).astype(dtype).astype(np.float64)
    return np.moveaxis((codes * scale).reshape(v.shape), -1, axis)


WIDE = False


def mx_kscale(k):
    if not WIDE:
        return np.ones(k)
    levels = np.array([30, -30])
    if k % 512:
        return np.exp2(np.random.permutation(np.resize(levels, k // 32))).repeat(32)
    a = np.empty((k // 512, 16))
    for p in range(k // 512):
        a[p, :8] = np.random.permutation(np.resize(levels, 8))
        for g in range(8):
            far = levels[np.abs(levels - a[p, g]) >= 10]
            a[p, g + 8] = far[np.random.randint(len(far))]
    return np.exp2(a.ravel()).repeat(32)


BF16 = ml_dtypes.bfloat16


def bf(x):
    return np.asarray(x, np.float32).astype(BF16)


def f64(x):
    return np.asarray(x).astype(np.float64)


S, E, H, DH = 1024, 1024, 16, 64
W = H * DH


def rotate_half(t):
    return np.stack((-t[..., 1::2], t[..., ::2]), axis=-1).reshape(t.shape)


def setup_inputs():
    s = mx_kscale(E)
    return {"hidden_states": bf(np.random.standard_normal((S, E)) * s),
            "cos": bf(np.random.uniform(size=(S, DH))),
            "sin": bf(np.random.uniform(size=(S, DH))),
            "w_qkv": bf(np.random.standard_normal((E, 3 * W)) * 2.0 / np.sqrt(E) / s[:, None]),
            "b_qkv": bf(np.random.standard_normal(3 * W) * 0.3)}


def reference(hidden_states, cos, sin, w_qkv, b_qkv):
    qkv = ((mxq(f64(hidden_states), 1, "e5m2") @ mxq(f64(w_qkv), 0, "e5m2")) + f64(b_qkv)).reshape(S, 3, H, DH)
    q, k, v = qkv[:, 0], qkv[:, 1], qkv[:, 2]
    c = f64(cos)[:, None, :]
    sn = f64(sin)[:, None, :]
    q_rot = q * c + rotate_half(q) * sn
    k_rot = k * c + rotate_half(k) * sn
    return q_rot, k_rot, v

@@ -1,0 +1,379 @@
+from contextlib import ExitStack
+
+import concourse.mybir as mybir
+from concourse.masks import make_identity
+
+S, E, H, DH = 1024, 1024, 16, 64
+W = H * DH
+FLOPS = 2 * S * E * 3 * W
+
+F32 = mybir.dt.float32
+BF16 = mybir.dt.bfloat16
+U32 = mybir.dt.uint32
+U8 = mybir.dt.uint8
+FP8X4 = mybir.dt.float8_e5m2_x4
+ADD = mybir.AluOpType.add
+MULT = mybir.AluOpType.mult
+
+P = 128
+PACK = 4
+K_PASS = P * PACK
+PASSES = E // K_PASS
+TILES = S // P
+BLK = 512
+CH_TILES = BLK // P
+PIECE = 128
+
+HALF = TILES // 2
+ROT_BLOCKS = (0, 1, 2, 3)
+V_BLOCKS = (4, 5)
+W_ORDER = (0, 1, 4, 2, 3, 5)
+BLOCK_UNITS = (("ch", 0, 0), ("ch", 1, 0), ("tok", 0, 1), ("ch", 2, 0), ("ch", 0, 1), ("ch", 3, 0), ("tok", 1, 1), ("ch", 1, 1))
+LAG = 2
+PIECES = (3, 4)
+V_START = (6, 14)
+GP_SHARE = 2
+SUMS_BANKS = 5
+HEAD_SPLIT = 352
+Q_DELAY = 2
+EARLY = (2, 4, 4)
+V_LAST = 2
+V_FIRST = 1
+STORE_LAG = 2
+GP_STEPS = (10, 16)
+
+
+def tile_arlowvisionattention_pa_kernel(tc, hidden_states, cos, sin, w_qkv, b_qkv, out_0, out_1, out_2):
+    nc = tc.nc
+    outs = [o.rearrange("(p j) h d -> p j (h d)", j=TILES) for o in (out_0, out_1, out_2)]
+    x_rows = hidden_states.rearrange("(p j) k -> p j k", j=TILES)
+
+    with ExitStack() as ctx:
+        keep = ctx.enter_context(tc.tile_pool(name="keep", bufs=1))
+        w_raw_pool = ctx.enter_context(tc.tile_pool(name="w_raw", bufs=8))
+        w_grouped_pool = ctx.enter_context(tc.tile_pool(name="w_grouped", bufs=4))
+        work = ctx.enter_context(tc.tile_pool(name="work", bufs=3))
+        result_pool = ctx.enter_context(tc.tile_pool(name="result", bufs=3))
+        sums_pool = ctx.enter_context(tc.psum_pool(name="sums", bufs=SUMS_BANKS))
+        turned_pool = ctx.enter_context(tc.psum_pool(name="turned", bufs=8 - SUMS_BANKS))
+        ctx.enter_context(tc.manual_schedule())
+
+        ident = keep.tile([P, P], F32)
+        ident_bf = keep.tile([P, P], BF16)
+        pair_swap = keep.tile([P, P], F32)
+        signs = keep.tile([P, 2], BF16)
+        bias_rows = keep.tile([P, P], BF16)
+        bias_cols = keep.tile([P, 2 * W // P], F32)
+        bias_all = keep.tile([P, 3 * W], BF16)
+        cos_tok = keep.tile([P, TILES, DH], BF16)
+        sin_raw = keep.tile([P, TILES, DH], BF16)
+        sin_tok = keep.tile([P, TILES, DH], BF16)
+        cos_twice = keep.tile([P, TILES, 2, DH], BF16)
+        sin_twice = keep.tile([P, TILES, 2, DH], BF16)
+        cos_ch = keep.tile([P, S], BF16)
+        sin_ch = keep.tile([P, S], BF16)
+        x_raw = keep.tile([P, TILES, E], BF16)
+        x_grouped = keep.tile([P, PASSES, TILES, P, PACK], BF16, align_bytes=64)
+        x_codes = keep.tile([P, PASSES, S], U32, align_bytes=64)
+        x_scales = keep.tile([P, PASSES, S], U8, align_bytes=64)
+        w_codes = keep.tile([P, 6, PASSES, BLK], U32, align_bytes=64)
+        w_scales = keep.tile([P, 6, PASSES, BLK], U8, align_bytes=64)
+
+        w_raw, w_grouped, results, products = {}, {}, {}, {}
+
+        def load_w(blk, g):
+            raw = w_raw_pool.tile([P, PACK, BLK], BF16, name="raw")
+            rows = w_qkv[g * K_PASS : (g + 1) * K_PASS, blk * BLK : (blk + 1) * BLK]
+            nc.sync.dma_start(out=raw[:], in_=rows.rearrange("(p t) n -> p t n", t=PACK))
+            w_raw[blk, g] = raw
+
+        def load_x(pair):
+            tiles = slice(2 * pair, 2 * pair + 2)
+            nc.sync.dma_start(out=x_raw[:, tiles, :], in_=x_rows[:, tiles, :])
+
+        def interleave_w(copy, blk, g, n0, n1):
+            if n0 == 0:
+                w_grouped[blk, g] = w_grouped_pool.tile([P, BLK, PACK], BF16, name="grouped", align_bytes=64)
+            copy(
+                out=w_grouped[blk, g][:, n0:n1, :].rearrange("p (c i) t -> p c t i", i=4),
+                in_=w_raw[blk, g][:, :, n0:n1].rearrange("p t (c i) -> p c t i", i=4),
+            )
+
+        def quantize_w(blk, g):
+            nc.vector.quantize_mx(
+                out=w_codes[:, blk, g, :].bitcast(FP8X4),
+                scales=w_scales[:, blk, g, :],
+                in_=w_grouped[blk, g][:].rearrange("p n t -> p (n t)"),
+            )
+
+        def turn_x(j, copy):
+            words = x_raw[:, j, :].bitcast(F32)
+            turned = turned_pool.tile([P, PASSES, 2, P], F32, name="turned")
+            for g in range(PASSES):
+                for u in range(2):
+                    nc.tensor.transpose(turned[:, g, u, :], words[:, 2 * P * g + u : 2 * P * (g + 1) : 2], ident[:])
+            dst = x_grouped[:, :, j, :, :].rearrange("p g r t -> p g (r t)").bitcast(F32)
+            copy(
+                out=dst.rearrange("p g (r u) -> p g r u", u=2), in_=turned[:].rearrange("p g u r -> p g r u")
+            )
+
+        def quantize_x(pair):
+            tokens = slice(2 * pair * P, (2 * pair + 2) * P)
+            for g in range(PASSES):
+                nc.vector.quantize_mx(
+                    out=x_codes[:, g, tokens].bitcast(FP8X4),
+                    scales=x_scales[:, g, tokens],
+                    in_=x_grouped[:, g, 2 * pair : 2 * pair + 2, :, :].rearrange("p j r t -> p (j r t)"),
+                )
+
+        def project(dst, blk, channels, tokens, tokens_on_partitions):
+            for g in range(PASSES):
+                w_side = (w_codes[:, blk, g, channels].bitcast(FP8X4), w_scales[:, blk, g, channels])
+                x_side = (x_codes[:, g, tokens].bitcast(FP8X4), x_scales[:, g, tokens])
+                fixed, moving = (x_side, w_side) if tokens_on_partitions else (w_side, x_side)
+                nc.tensor.matmul_mx(
+                    out=dst,
+                    lhsT=fixed[0],
+                    lhsT_scale=fixed[1],
+                    rhs=moving[0],
+                    rhs_scale=moving[1],
+                    start=(g == 0),
+                    stop=(g == PASSES - 1),
+                )
+
+        def project_token_tile(blk, j):
+            sums = sums_pool.tile([P, BLK], F32, name="sums")
+            project(sums[:], blk, slice(0, BLK), slice(j * P, (j + 1) * P), True)
+            return sums
+
+        def result_of(blk):
+            if blk not in results:
+                results[blk] = result_pool.tile([P, TILES, BLK], F32, name="result")
+            return results[blk]
+
+        def store(blk, j0, j1, c0, c1):
+            first_col = (blk % 2) * BLK
+            nc.sync.dma_start(
+                out=outs[blk // 2][:, j0:j1, first_col + c0 : first_col + c1], in_=results[blk][:, j0:j1, c0:c1]
+            )
+
+        def value_tile(blk, j, on_gpsimd):
+            sums = project_token_tile(blk, j)
+            bias = bias_all[:, blk * BLK : (blk + 1) * BLK]
+            if on_gpsimd:
+                plain = work.tile([P, BLK], F32, bufs=2)
+                nc.scalar.copy(out=plain[:], in_=sums[:])
+                nc.gpsimd.tensor_tensor(out=result_of(blk)[:, j, :], in0=plain[:], in1=bias, op=ADD)
+            else:
+                nc.vector.tensor_tensor(out=result_of(blk)[:, j, :], in0=sums[:], in1=bias, op=ADD)
+
+        def spread_bias(which):
+            spread = turned_pool.tile([P, W], BF16, name="turned")
+            for r in range(W // P):
+                row = which * (W // P) + r
+                nc.tensor.matmul(
+                    spread[:, r * P : (r + 1) * P],
+                    lhsT=ident_bf[:, row : row + 1].to_broadcast([P, P]),
+                    rhs=bias_rows[:],
+                    start=True,
+                    stop=True,
+                )
+            nc.scalar.copy(out=bias_all[:, which * W : (which + 1) * W], in_=spread[:])
+
+        def turn_table(twice, table):
+            turned = turned_pool.tile([P, S], BF16, name="turned")
+            for j in range(TILES):
+                nc.tensor.matmul(
+                    turned[:, j * P : (j + 1) * P],
+                    lhsT=twice[:, j, :, :].rearrange("p r d -> p (r d)"),
+                    rhs=ident_bf[:],
+                    start=True,
+                    stop=True,
+                )
+            nc.scalar.copy(out=table[:], in_=turned[:])
+
+        def multiply_tables(sums, ch_tile, table_cols, with_cos, with_sin):
+            bias = bias_cols[:, ch_tile : ch_tile + 1]
+            for dst, table in ((with_cos, cos_ch), (with_sin, sin_ch)):
+                nc.vector.scalar_tensor_tensor(
+                    out=dst, in0=sums, scalar=bias, in1=table[:, table_cols], op0=ADD, op1=MULT
+                )
+
+        def turn_and_add(dst, with_cos, with_sin):
+            nc.tensor.matmul(dst, lhsT=with_cos, rhs=ident[:], start=True, stop=False, is_transpose=True)
+            nc.tensor.matmul(dst, lhsT=with_sin, rhs=pair_swap[:], start=False, stop=True, is_transpose=True)
+
+        def channel_unit(blk, c, half):
+            tokens = slice(half * HALF * P, (half + 1) * HALF * P)
+            sums = sums_pool.tile([P, HALF * P], F32, name="sums")
+            project(sums[:], blk, slice(c * P, (c + 1) * P), tokens, False)
+            with_cos = work.tile([P, HALF * P], F32, bufs=2 * LAG + 2)
+            with_sin = work.tile([P, HALF * P], F32, bufs=2 * LAG + 2)
+            multiply_tables(sums[:], blk * CH_TILES + c, tokens, with_cos[:], with_sin[:])
+            products[blk, c, half] = (with_cos, with_sin)
+
+        def finish_channel_unit(blk, c, half):
+            with_cos, with_sin = products.pop((blk, c, half))
+            turned = turned_pool.tile([P, HALF, P], F32, name="turned")
+            for s in range(HALF):
+                turn_and_add(turned[:, s, :], with_cos[:, s * P : (s + 1) * P], with_sin[:, s * P : (s + 1) * P])
+            nc.scalar.copy(out=result_of(blk)[:, half * HALF : (half + 1) * HALF, c * P : (c + 1) * P], in_=turned[:])
+            if c % 2 == 1:
+                store(blk, half * HALF, (half + 1) * HALF, (c - 1) * P, (c + 1) * P)
+
+        def token_unit(blk, pair):
+            j0 = HALF + 2 * pair
+            cols = slice(BLK // 2, BLK)
+            sums = sums_pool.tile([P, 2, BLK // 2], F32, name="sums")
+            for i in range(2):
+                project(sums[:, i, :], blk, cols, slice((j0 + i) * P, (j0 + i + 1) * P), True)
+            biased = work.tile([P, 2, BLK // 2], F32, bufs=2)
+            tok_cos = work.tile([P, 2, BLK // 2], F32, bufs=2)
+            tok_sin = work.tile([P, 2, BLK // 2], F32, bufs=2)
+            bias = bias_all[:, blk * BLK + BLK // 2 : (blk + 1) * BLK]
+            nc.vector.tensor_tensor(
+                out=biased[:], in0=sums[:], in1=bias.unsqueeze(1).to_broadcast([P, 2, BLK // 2]), op=ADD
+            )
+            heads = BLK // 2 // DH
+            for dst, table in ((tok_cos, cos_tok), (tok_sin, sin_tok)):
+                nc.gpsimd.tensor_tensor(
+                    out=dst[:].rearrange("p j (h d) -> p j h d", d=DH),
+                    in0=biased[:].rearrange("p j (h d) -> p j h d", d=DH),
+                    in1=table[:, j0 : j0 + 2, :].unsqueeze(2).to_broadcast([P, 2, heads, DH]),
+                    op=MULT,
+                )
+            nc.gpsimd.tensor_tensor(
+                out=result_of(blk)[:, j0 : j0 + 2, cols].rearrange("p j (n e) -> p j n e", e=2),
+                in0=tok_cos[:].rearrange("p j (n e) -> p j n e", e=2),
+                in1=tok_sin[:].rearrange("p j (n e) -> p j n e", e=2)[:, :, :, ::-1],
+                op=ADD,
+            )
+
+        nc.vector.memset(bias_rows[:], 0.0)
+        nc.scalar.dma_start(out=sin_raw[:], in_=sin.rearrange("(p j) d -> p j d", j=TILES))
+        nc.scalar.dma_start(out=cos_tok[:], in_=cos.rearrange("(p j) d -> p j d", j=TILES))
+        nc.scalar.dma_start(out=bias_rows[0 : 3 * W // P, :], in_=b_qkv.rearrange("(r c) -> r c", c=P))
+        make_identity(nc, ident[:])
+        nc.vector.memset(signs[:, 0:1], 1.0)
+        nc.vector.memset(signs[:, 1:2], -1.0)
+        nc.vector.tensor_copy(out=ident_bf[:], in_=ident[:])
+        nc.vector.tensor_copy(
+            out=pair_swap[:].rearrange("p (n e) -> p n e", e=2),
+            in_=ident[:].rearrange("p (n e) -> p n e", e=2)[:, :, ::-1],
+        )
+
+        first = W_ORDER[0]
+        load_w(first, 0)
+        load_x(0)
+        load_x(1)
+        load_w(first, 1)
+        load_x(2)
+        load_w(W_ORDER[1], 0)
+        load_x(3)
+        load_w(W_ORDER[1], 1)
+        for blk in W_ORDER[2:4]:
+            load_w(blk, 0)
+            load_w(blk, 1)
+
+        nc.vector.tensor_tensor(
+            out=sin_tok[:].rearrange("p j (n e) -> p (j n) e", e=2),
+            in0=sin_raw[:].rearrange("p j (n e) -> p (j n) e", e=2)[:, :, ::-1],
+            in1=signs[:].unsqueeze(1).to_broadcast([P, TILES * DH // 2, 2]),
+            op=MULT,
+        )
+        spread_bias(0)
+        bias_turned = turned_pool.tile([P, P], BF16, name="turned")
+        nc.tensor.transpose(bias_turned[:], bias_rows[:], ident_bf[:])
+        interleave_w(nc.vector.tensor_copy, first, 0, 0, BLK)
+        nc.scalar.copy(out=bias_cols[:], in_=bias_turned[:, 0 : 2 * W // P])
+        nc.vector.tensor_copy(out=cos_twice[:], in_=cos_tok[:].unsqueeze(2).to_broadcast([P, TILES, 2, DH]))
+        quantize_w(first, 0)
+        nc.vector.tensor_copy(out=sin_twice[:], in_=sin_tok[:].unsqueeze(2).to_broadcast([P, TILES, 2, DH]))
+        turn_x(0, nc.scalar.copy)
+        turn_x(1, nc.vector.tensor_copy)
+        turn_table(cos_twice, cos_ch)
+        turn_x(2, nc.scalar.copy)
+        turn_x(3, nc.scalar.copy)
+        quantize_x(0)
+        turn_table(sin_twice, sin_ch)
+        interleave_w(nc.vector.tensor_copy, first, 1, 0, BLK)
+        quantize_x(1)
+        quantize_w(first, 1)
+        for blk in W_ORDER[4:]:
+            load_w(blk, 0)
+            load_w(blk, 1)
+        turn_x(4, nc.scalar.copy)
+        turn_x(5, nc.scalar.copy)
+        quantize_x(2)
+
+        halves = [(blk, g) for blk in W_ORDER[1:] for g in range(PASSES)]
+        pieces = [(blk, g, n0) for blk, g in halves for n0 in range(0, BLK, PIECE)]
+        grouped_at = []
+
+        def next_pieces(count, step):
+            for i in range(min(count, len(pieces))):
+                blk, g, n0 = pieces.pop(0)
+                interleave_w(nc.scalar.copy, blk, g, n0, n0 + PIECE)
+                if n0 + PIECE == BLK:
+                    grouped_at.append((step, blk, g))
+
+        def quantize_grouped(step):
+            if grouped_at and grouped_at[0][0] + Q_DELAY <= step:
+                quantize_w(*grouped_at.pop(0)[1:])
+
+        units = [(kind, blk, a, b) for blk in ROT_BLOCKS for kind, a, b in BLOCK_UNITS]
+        steps = [units[i : i + 2] for i in range(0, len(units), 2)]
+        pending_stores = []
+
+        def value_unit(blk, j, step):
+            on_gpsimd = GP_STEPS[0] <= step < GP_STEPS[1] and j % GP_SHARE == 0
+            value_tile(blk, j, on_gpsimd)
+            if on_gpsimd:
+                pending_stores.append((step, blk, j, j + 1, 0, BLK))
+            else:
+                store(blk, j, j + 1, 0, BLK)
+
+        def finish_step(step, now):
+            done = [u for u in steps[step] if u[0] == "ch"]
+            next_pieces(PIECES[now % 2] - len(done), now)
+            for kind, blk, a, b in done:
+                finish_channel_unit(blk, a, b)
+                next_pieces(1, now)
+
+        first_values = list(range(TILES))
+        last_values = list(range(TILES))
+        for step in range(len(steps) + LAG):
+            for kind, blk, a, b in steps[step] if step < len(steps) else []:
+                if kind == "ch":
+                    channel_unit(blk, a, b)
+                else:
+                    token_unit(blk, a)
+                    quantize_grouped(step)
+                    quantize_grouped(step)
+                    pending_stores.append((step, blk, HALF + 2 * a, HALF + 2 * a + 2, BLK // 2, BLK))
+            if step == 0:
+                next_pieces(EARLY[0], step)
+                turn_x(6, nc.scalar.copy)
+                turn_x(7, nc.scalar.copy)
+                quantize_x(3)
+                next_pieces(EARLY[1], step)
+            if step == 1:
+                next_pieces(EARLY[2], step)
+            if step == 3:
+                spread_bias(2)
+            if step == 5:
+                spread_bias(1)
+            if step >= V_START[0]:
+                for j in first_values[:V_FIRST]:
+                    value_unit(V_BLOCKS[0], first_values.pop(0), step)
+            if step >= V_START[1]:
+                for j in last_values[:V_LAST]:
+                    value_unit(V_BLOCKS[1], last_values.pop(0), step)
+            if step >= LAG:
+                finish_step(step - LAG, step)
+            while pending_stores and pending_stores[0][0] + STORE_LAG <= step:
+                store(*pending_stores.pop(0)[1:])
+        for j in last_values:
+            value_unit(V_BLOCKS[1], j, len(steps) + LAG)
+        for args in pending_stores:
+            store(*args[1:])

@@ -28,19 +28,29 @@ HALF = TILES // 2
 ROT_BLOCKS = (0, 1, 2, 3)
 V_BLOCKS = (4, 5)
 W_ORDER = (0, 1, 4, 2, 3, 5)
-BLOCK_UNITS = (("ch", 0, 0), ("ch", 1, 0), ("tok", 0, 1), ("ch", 2, 0), ("ch", 0, 1), ("ch", 3, 0), ("tok", 1, 1), ("ch", 1, 1))
+TOKEN_UNITS = (2, 2, 2, 2)
+STEP_UNITS = 2
+BIASED_BUFS = 4
 LAG = 2
 PIECES = (3, 4)
 V_START = (6, 14)
 GP_SHARE = 2
 SUMS_BANKS = 5
-HEAD_SPLIT = 352
-Q_DELAY = 2
-EARLY = (2, 4, 4)
+HEAD_SPLIT = 384
+Q_DELAY = 1
+EARLY = (0, 3, 3)
 V_LAST = 2
 V_FIRST = 1
-STORE_LAG = 2
-GP_STEPS = (10, 16)
+STORE_LAG = 1
+GP_STEPS = (6, 15)
+FINE_FROM = 1
+TOK_SLOT = 0
+Q_BEFORE = 0
+G_BUFS = 2
+TAIL_FIRST = 1
+HEAD_ORDER = 0
+V_TAKE = (0, 12, 2)
+SPREADS = (3, 5)
 
 
 def tile_arlowvisionattention_pa_kernel(tc, hidden_states, cos, sin, w_qkv, b_qkv, out_0, out_1, out_2):
@@ -51,7 +61,7 @@ def tile_arlowvisionattention_pa_kernel(tc, hidden_states, cos, sin, w_qkv, b_qk
     with ExitStack() as ctx:
         keep = ctx.enter_context(tc.tile_pool(name="keep", bufs=1))
         w_raw_pool = ctx.enter_context(tc.tile_pool(name="w_raw", bufs=8))
-        w_grouped_pool = ctx.enter_context(tc.tile_pool(name="w_grouped", bufs=4))
+        w_grouped_pool = ctx.enter_context(tc.tile_pool(name="w_grouped", bufs=G_BUFS))
         work = ctx.enter_context(tc.tile_pool(name="work", bufs=3))
         result_pool = ctx.enter_context(tc.tile_pool(name="result", bufs=3))
         sums_pool = ctx.enter_context(tc.psum_pool(name="sums", bufs=SUMS_BANKS))
@@ -65,13 +75,13 @@ def tile_arlowvisionattention_pa_kernel(tc, hidden_states, cos, sin, w_qkv, b_qk
         bias_rows = keep.tile([P, P], BF16)
         bias_cols = keep.tile([P, 2 * W // P], F32)
         bias_all = keep.tile([P, 3 * W], BF16)
-        cos_tok = keep.tile([P, TILES, DH], BF16)
+        tables_tok = keep.tile([P, 2, TILES, DH], BF16)
         sin_raw = keep.tile([P, TILES, DH], BF16)
-        sin_tok = keep.tile([P, TILES, DH], BF16)
         cos_twice = keep.tile([P, TILES, 2, DH], BF16)
         sin_twice = keep.tile([P, TILES, 2, DH], BF16)
-        cos_ch = keep.tile([P, S], BF16)
-        sin_ch = keep.tile([P, S], BF16)
+        tables_ch = keep.tile([P, 2, S], BF16)
+        cos_tok, sin_tok = tables_tok[:, 0, :, :], tables_tok[:, 1, :, :]
+        cos_ch, sin_ch = tables_ch[:, 0, :], tables_ch[:, 1, :]
         x_raw = keep.tile([P, TILES, E], BF16)
         x_grouped = keep.tile([P, PASSES, TILES, P, PACK], BF16, align_bytes=64)
         x_codes = keep.tile([P, PASSES, S], U32, align_bytes=64)
@@ -92,18 +102,18 @@ def tile_arlowvisionattention_pa_kernel(tc, hidden_states, cos, sin, w_qkv, b_qk
             nc.sync.dma_start(out=x_raw[:, tiles, :], in_=x_rows[:, tiles, :])
 
         def interleave_w(copy, blk, g, n0, n1):
-            if n0 == 0:
-                w_grouped[blk, g] = w_grouped_pool.tile([P, BLK, PACK], BF16, name="grouped", align_bytes=64)
+            if n0 == 0 and g == 0:
+                w_grouped[blk] = w_grouped_pool.tile([P, PASSES, BLK, PACK], BF16, name="grouped", align_bytes=64)
             copy(
-                out=w_grouped[blk, g][:, n0:n1, :].rearrange("p (c i) t -> p c t i", i=4),
+                out=w_grouped[blk][:, g, n0:n1, :].rearrange("p (c i) t -> p c t i", i=4),
                 in_=w_raw[blk, g][:, :, n0:n1].rearrange("p t (c i) -> p c t i", i=4),
             )
 
-        def quantize_w(blk, g):
+        def quantize_w(blk, passes):
             nc.vector.quantize_mx(
-                out=w_codes[:, blk, g, :].bitcast(FP8X4),
-                scales=w_scales[:, blk, g, :],
-                in_=w_grouped[blk, g][:].rearrange("p n t -> p (n t)"),
+                out=w_codes[:, blk, passes, :].rearrange("p g n -> p (g n)").bitcast(FP8X4),
+                scales=w_scales[:, blk, passes, :].rearrange("p g n -> p (g n)"),
+                in_=w_grouped[blk][:, passes, :, :].rearrange("p g n t -> p (g n t)"),
             )
 
         def turn_x(j, copy):
@@ -190,14 +200,7 @@ def tile_arlowvisionattention_pa_kernel(tc, hidden_states, cos, sin, w_qkv, b_qk
                     start=True,
                     stop=True,
                 )
-            nc.scalar.copy(out=table[:], in_=turned[:])
-
-        def multiply_tables(sums, ch_tile, table_cols, with_cos, with_sin):
-            bias = bias_cols[:, ch_tile : ch_tile + 1]
-            for dst, table in ((with_cos, cos_ch), (with_sin, sin_ch)):
-                nc.vector.scalar_tensor_tensor(
-                    out=dst, in0=sums, scalar=bias, in1=table[:, table_cols], op0=ADD, op1=MULT
-                )
+            nc.scalar.copy(out=table, in_=turned[:])
 
         def turn_and_add(dst, with_cos, with_sin):
             nc.tensor.matmul(dst, lhsT=with_cos, rhs=ident[:], start=True, stop=False, is_transpose=True)
@@ -207,30 +210,37 @@ def tile_arlowvisionattention_pa_kernel(tc, hidden_states, cos, sin, w_qkv, b_qk
             tokens = slice(half * HALF * P, (half + 1) * HALF * P)
             sums = sums_pool.tile([P, HALF * P], F32, name="sums")
             project(sums[:], blk, slice(c * P, (c + 1) * P), tokens, False)
-            with_cos = work.tile([P, HALF * P], F32, bufs=2 * LAG + 2)
-            with_sin = work.tile([P, HALF * P], F32, bufs=2 * LAG + 2)
-            multiply_tables(sums[:], blk * CH_TILES + c, tokens, with_cos[:], with_sin[:])
-            products[blk, c, half] = (with_cos, with_sin)
+            product = work.tile([P, 2, HALF * P], F32, bufs=STEP_UNITS * (LAG + 1))
+            nc.vector.scalar_tensor_tensor(
+                out=product[:],
+                in0=sums[:].unsqueeze(1).to_broadcast([P, 2, HALF * P]),
+                scalar=bias_cols[:, blk * CH_TILES + c : blk * CH_TILES + c + 1],
+                in1=tables_ch[:, :, tokens],
+                op0=ADD,
+                op1=MULT,
+            )
+            products[blk, c, half] = product
 
         def finish_channel_unit(blk, c, half):
-            with_cos, with_sin = products.pop((blk, c, half))
+            product = products.pop((blk, c, half))
             turned = turned_pool.tile([P, HALF, P], F32, name="turned")
             for s in range(HALF):
-                turn_and_add(turned[:, s, :], with_cos[:, s * P : (s + 1) * P], with_sin[:, s * P : (s + 1) * P])
+                turn_and_add(turned[:, s, :], product[:, 0, s * P : (s + 1) * P], product[:, 1, s * P : (s + 1) * P])
             nc.scalar.copy(out=result_of(blk)[:, half * HALF : (half + 1) * HALF, c * P : (c + 1) * P], in_=turned[:])
             if c % 2 == 1:
                 store(blk, half * HALF, (half + 1) * HALF, (c - 1) * P, (c + 1) * P)
 
-        def token_unit(blk, pair):
+        def token_unit(blk, pair, col_half, before_bias):
             j0 = HALF + 2 * pair
-            cols = slice(BLK // 2, BLK)
+            cols = slice(col_half * BLK // 2, (col_half + 1) * BLK // 2)
             sums = sums_pool.tile([P, 2, BLK // 2], F32, name="sums")
             for i in range(2):
                 project(sums[:, i, :], blk, cols, slice((j0 + i) * P, (j0 + i + 1) * P), True)
-            biased = work.tile([P, 2, BLK // 2], F32, bufs=2)
-            tok_cos = work.tile([P, 2, BLK // 2], F32, bufs=2)
-            tok_sin = work.tile([P, 2, BLK // 2], F32, bufs=2)
-            bias = bias_all[:, blk * BLK + BLK // 2 : (blk + 1) * BLK]
+            before_bias()
+            biased = work.tile([P, 2, BLK // 2], F32, bufs=BIASED_BUFS)
+            tok_cos = work.tile([P, 2, BLK // 2], F32, bufs=1)
+            tok_sin = work.tile([P, 2, BLK // 2], F32, bufs=1)
+            bias = bias_all[:, blk * BLK : (blk + 1) * BLK][:, cols]
             nc.vector.tensor_tensor(
                 out=biased[:], in0=sums[:], in1=bias.unsqueeze(1).to_broadcast([P, 2, BLK // 2]), op=ADD
             )
@@ -250,9 +260,14 @@ def tile_arlowvisionattention_pa_kernel(tc, hidden_states, cos, sin, w_qkv, b_qk
             )
 
         nc.vector.memset(bias_rows[:], 0.0)
-        nc.scalar.dma_start(out=sin_raw[:], in_=sin.rearrange("(p j) d -> p j d", j=TILES))
-        nc.scalar.dma_start(out=cos_tok[:], in_=cos.rearrange("(p j) d -> p j d", j=TILES))
-        nc.scalar.dma_start(out=bias_rows[0 : 3 * W // P, :], in_=b_qkv.rearrange("(r c) -> r c", c=P))
+        bias_src = b_qkv.rearrange("(r c) -> r c", c=P)
+        rot_rows = 2 * W // P
+        if HEAD_ORDER:
+            load_w(W_ORDER[0], 0)
+        nc.sync.dma_start(out=sin_raw[:], in_=sin.rearrange("(p j) d -> p j d", j=TILES))
+        nc.sync.dma_start(out=cos_tok, in_=cos.rearrange("(p j) d -> p j d", j=TILES))
+        nc.sync.dma_start(out=bias_rows[0:rot_rows, :], in_=bias_src[0:rot_rows, :])
+        nc.sync.dma_start(out=bias_rows[rot_rows : 3 * W // P, :], in_=bias_src[rot_rows:, :])
         make_identity(nc, ident[:])
         nc.vector.memset(signs[:, 0:1], 1.0)
         nc.vector.memset(signs[:, 1:2], -1.0)
@@ -263,20 +278,23 @@ def tile_arlowvisionattention_pa_kernel(tc, hidden_states, cos, sin, w_qkv, b_qk
         )
 
         first = W_ORDER[0]
-        load_w(first, 0)
+        if not HEAD_ORDER:
+            load_w(first, 0)
         load_x(0)
         load_x(1)
         load_w(first, 1)
         load_x(2)
-        load_w(W_ORDER[1], 0)
         load_x(3)
+        load_w(W_ORDER[1], 0)
         load_w(W_ORDER[1], 1)
         for blk in W_ORDER[2:4]:
             load_w(blk, 0)
             load_w(blk, 1)
 
+        if HEAD_ORDER:
+            interleave_w(nc.vector.tensor_copy, first, 0, 0, BLK)
         nc.vector.tensor_tensor(
-            out=sin_tok[:].rearrange("p j (n e) -> p (j n) e", e=2),
+            out=sin_tok.rearrange("p j (n e) -> p (j n) e", e=2),
             in0=sin_raw[:].rearrange("p j (n e) -> p (j n) e", e=2)[:, :, ::-1],
             in1=signs[:].unsqueeze(1).to_broadcast([P, TILES * DH // 2, 2]),
             op=MULT,
@@ -284,27 +302,30 @@ def tile_arlowvisionattention_pa_kernel(tc, hidden_states, cos, sin, w_qkv, b_qk
         spread_bias(0)
         bias_turned = turned_pool.tile([P, P], BF16, name="turned")
         nc.tensor.transpose(bias_turned[:], bias_rows[:], ident_bf[:])
-        interleave_w(nc.vector.tensor_copy, first, 0, 0, BLK)
+        nc.vector.tensor_copy(out=cos_twice[:], in_=cos_tok.unsqueeze(2).to_broadcast([P, TILES, 2, DH]))
+        nc.vector.tensor_copy(out=sin_twice[:], in_=sin_tok.unsqueeze(2).to_broadcast([P, TILES, 2, DH]))
         nc.scalar.copy(out=bias_cols[:], in_=bias_turned[:, 0 : 2 * W // P])
-        nc.vector.tensor_copy(out=cos_twice[:], in_=cos_tok[:].unsqueeze(2).to_broadcast([P, TILES, 2, DH]))
-        quantize_w(first, 0)
-        nc.vector.tensor_copy(out=sin_twice[:], in_=sin_tok[:].unsqueeze(2).to_broadcast([P, TILES, 2, DH]))
-        turn_x(0, nc.scalar.copy)
-        turn_x(1, nc.vector.tensor_copy)
         turn_table(cos_twice, cos_ch)
+        if not HEAD_ORDER:
+            interleave_w(nc.vector.tensor_copy, first, 0, 0, BLK)
+        turn_table(sin_twice, sin_ch)
+        turn_x(0, nc.scalar.copy)
+        quantize_w(first, slice(0, 1))
+        turn_x(1, nc.vector.tensor_copy)
+        spread_bias(2)
         turn_x(2, nc.scalar.copy)
         turn_x(3, nc.scalar.copy)
         quantize_x(0)
-        turn_table(sin_twice, sin_ch)
-        interleave_w(nc.vector.tensor_copy, first, 1, 0, BLK)
+        interleave_w(nc.vector.tensor_copy, first, 1, 0, HEAD_SPLIT)
+        interleave_w(nc.scalar.copy, first, 1, HEAD_SPLIT, BLK)
+        spread_bias(1)
         quantize_x(1)
-        quantize_w(first, 1)
+        quantize_w(first, slice(1, 2))
         for blk in W_ORDER[4:]:
             load_w(blk, 0)
             load_w(blk, 1)
         turn_x(4, nc.scalar.copy)
         turn_x(5, nc.scalar.copy)
-        quantize_x(2)
 
         halves = [(blk, g) for blk in W_ORDER[1:] for g in range(PASSES)]
         pieces = [(blk, g, n0) for blk, g in halves for n0 in range(0, BLK, PIECE)]
@@ -314,15 +335,34 @@ def tile_arlowvisionattention_pa_kernel(tc, hidden_states, cos, sin, w_qkv, b_qk
             for i in range(min(count, len(pieces))):
                 blk, g, n0 = pieces.pop(0)
                 interleave_w(nc.scalar.copy, blk, g, n0, n0 + PIECE)
-                if n0 + PIECE == BLK:
-                    grouped_at.append((step, blk, g))
+                if n0 + PIECE == BLK and g == PASSES - 1:
+                    grouped_at.append((step, blk, slice(0, PASSES)))
+
+        def vector_pieces(step):
+            if pieces and V_TAKE[0] <= step < V_TAKE[1]:
+                blk, g, n0 = pieces[0]
+                count = min(V_TAKE[2], (BLK - n0) // PIECE)
+                del_count = [pieces.pop(0) for i in range(count)]
+                interleave_w(nc.vector.tensor_copy, blk, g, n0, n0 + count * PIECE)
+                if n0 + count * PIECE == BLK and g == PASSES - 1:
+                    grouped_at.append((step, blk, slice(0, PASSES)))
 
         def quantize_grouped(step):
             if grouped_at and grouped_at[0][0] + Q_DELAY <= step:
                 quantize_w(*grouped_at.pop(0)[1:])
 
-        units = [(kind, blk, a, b) for blk in ROT_BLOCKS for kind, a, b in BLOCK_UNITS]
-        steps = [units[i : i + 2] for i in range(0, len(units), 2)]
+        def block_units(blk, n_token):
+            first_half = [("ch", blk, c, 0) for c in range(CH_TILES)]
+            second_half = [("ch", blk, c, 1) for c in range(CH_TILES - n_token)]
+            by_token = [("tok", blk, pair, 1 - i) for i in range(n_token // 2) for pair in range(2)]
+            if n_token == 2:
+                second_half = [by_token[0], second_half[0], by_token[1], second_half[1]]
+            elif n_token == 4:
+                second_half = by_token
+            return first_half[:2] + [second_half[0], first_half[2], second_half[1], first_half[3]] + second_half[2:]
+
+        units = [u for blk, n in zip(ROT_BLOCKS, TOKEN_UNITS) for u in block_units(blk, n)]
+        steps = [units[i : i + STEP_UNITS] for i in range(0, len(units), STEP_UNITS)]
         pending_stores = []
 
         def value_unit(blk, j, step):
@@ -342,27 +382,28 @@ def tile_arlowvisionattention_pa_kernel(tc, hidden_states, cos, sin, w_qkv, b_qk
 
         first_values = list(range(TILES))
         last_values = list(range(TILES))
-        for step in range(len(steps) + LAG):
-            for kind, blk, a, b in steps[step] if step < len(steps) else []:
+        for step in range(len(steps)):
+            for kind, blk, a, b in steps[step]:
                 if kind == "ch":
                     channel_unit(blk, a, b)
                 else:
-                    token_unit(blk, a)
-                    quantize_grouped(step)
-                    quantize_grouped(step)
-                    pending_stores.append((step, blk, HALF + 2 * a, HALF + 2 * a + 2, BLK // 2, BLK))
+                    token_unit(blk, a, b, lambda: quantize_grouped(step) if Q_BEFORE else None)
+                    pending_stores.append((step, blk, HALF + 2 * a, HALF + 2 * a + 2, b * BLK // 2, (b + 1) * BLK // 2))
+                if (kind, blk, a, b) == units[0]:
+                    quantize_x(2)
+                if (kind, blk, a, b) == units[1]:
+                    turn_x(6, nc.scalar.copy)
+                    turn_x(7, nc.scalar.copy)
+                if (kind, blk, a, b) == units[2]:
+                    quantize_x(3)
+                if kind == "tok":
+                    if not Q_BEFORE:
+                        quantize_grouped(step)
+                    vector_pieces(step)
             if step == 0:
-                next_pieces(EARLY[0], step)
-                turn_x(6, nc.scalar.copy)
-                turn_x(7, nc.scalar.copy)
-                quantize_x(3)
                 next_pieces(EARLY[1], step)
             if step == 1:
                 next_pieces(EARLY[2], step)
-            if step == 3:
-                spread_bias(2)
-            if step == 5:
-                spread_bias(1)
             if step >= V_START[0]:
                 for j in first_values[:V_FIRST]:
                     value_unit(V_BLOCKS[0], first_values.pop(0), step)
@@ -371,9 +412,15 @@ def tile_arlowvisionattention_pa_kernel(tc, hidden_states, cos, sin, w_qkv, b_qk
                     value_unit(V_BLOCKS[1], last_values.pop(0), step)
             if step >= LAG:
                 finish_step(step - LAG, step)
-            while pending_stores and pending_stores[0][0] + STORE_LAG <= step:
-                store(*pending_stores.pop(0)[1:])
-        for j in last_values:
-            value_unit(V_BLOCKS[1], j, len(steps) + LAG)
+            for entry in [e for e in pending_stores if e[0] + STORE_LAG <= step]:
+                pending_stores.remove(entry)
+                store(*entry[1:])
+        for j in last_values[:TAIL_FIRST]:
+            value_unit(V_BLOCKS[1], j, len(steps))
+        for step in range(len(steps) - LAG, len(steps)):
+            finish_step(step, len(steps))
+        for j in last_values[TAIL_FIRST:-1]:
+            value_unit(V_BLOCKS[1], j, len(steps))
         for args in pending_stores:
             store(*args[1:])
+        value_unit(V_BLOCKS[1], last_values[-1], len(steps))

@@ -20,37 +20,26 @@ PACK = 4
 K_PASS = P * PACK
 PASSES = E // K_PASS
 TILES = S // P
-BLK = 512
-CH_TILES = BLK // P
-PIECE = 128
-
 HALF = TILES // 2
+BLK = 512
+BLOCKS = 3 * W // BLK
+CH_TILES = BLK // P
+BIAS_ROWS = 3 * W // P
+ROT_ROWS = 2 * W // P
+
 ROT_BLOCKS = (0, 1, 2, 3)
-V_BLOCKS = (4, 5)
-W_ORDER = (0, 1, 4, 2, 3, 5)
-TOKEN_UNITS = (2, 2, 2, 2)
+V_FIRST, V_LAST = 4, 5
+W_ORDER = (0, 1, V_FIRST, 2, 3, V_LAST)
+
 STEP_UNITS = 2
-BIASED_BUFS = 4
 LAG = 2
-PIECES = (3, 4)
-V_START = (6, 14)
-GP_SHARE = 2
 SUMS_BANKS = 5
-HEAD_SPLIT = 384
-Q_DELAY = 1
-EARLY = (0, 3, 3)
-V_LAST = 2
-V_FIRST = 1
-STORE_LAG = 1
-GP_STEPS = (6, 15)
-FINE_FROM = 1
-TOK_SLOT = 0
-Q_BEFORE = 0
-G_BUFS = 2
-TAIL_FIRST = 1
-HEAD_ORDER = 0
-V_TAKE = (0, 12, 2)
-SPREADS = (3, 5)
+PIECE = 128
+PIECES_PER_STEP = 4
+HELP_STEPS = (3, 5)
+HELP_PIECES = 2
+VALUES_PER_STEP = 2
+RAW_BUFS = 8
 
 
 def tile_arlowvisionattention_pa_kernel(tc, hidden_states, cos, sin, w_qkv, b_qkv, out_0, out_1, out_2):
@@ -60,9 +49,9 @@ def tile_arlowvisionattention_pa_kernel(tc, hidden_states, cos, sin, w_qkv, b_qk
 
     with ExitStack() as ctx:
         keep = ctx.enter_context(tc.tile_pool(name="keep", bufs=1))
-        w_raw_pool = ctx.enter_context(tc.tile_pool(name="w_raw", bufs=8))
-        w_grouped_pool = ctx.enter_context(tc.tile_pool(name="w_grouped", bufs=G_BUFS))
-        work = ctx.enter_context(tc.tile_pool(name="work", bufs=3))
+        w_raw_pool = ctx.enter_context(tc.tile_pool(name="w_raw", bufs=RAW_BUFS))
+        w_grouped_pool = ctx.enter_context(tc.tile_pool(name="w_grouped", bufs=2))
+        work = ctx.enter_context(tc.tile_pool(name="work", bufs=1))
         result_pool = ctx.enter_context(tc.tile_pool(name="result", bufs=3))
         sums_pool = ctx.enter_context(tc.psum_pool(name="sums", bufs=SUMS_BANKS))
         turned_pool = ctx.enter_context(tc.psum_pool(name="turned", bufs=8 - SUMS_BANKS))
@@ -73,21 +62,18 @@ def tile_arlowvisionattention_pa_kernel(tc, hidden_states, cos, sin, w_qkv, b_qk
         pair_swap = keep.tile([P, P], F32)
         signs = keep.tile([P, 2], BF16)
         bias_rows = keep.tile([P, P], BF16)
-        bias_cols = keep.tile([P, 2 * W // P], F32)
+        bias_cols = keep.tile([P, ROT_ROWS], F32)
         bias_all = keep.tile([P, 3 * W], BF16)
-        tables_tok = keep.tile([P, 2, TILES, DH], BF16)
         sin_raw = keep.tile([P, TILES, DH], BF16)
-        cos_twice = keep.tile([P, TILES, 2, DH], BF16)
-        sin_twice = keep.tile([P, TILES, 2, DH], BF16)
+        tables_tok = keep.tile([P, 2, TILES, DH], BF16)
+        tables_twice = keep.tile([P, 2, TILES, 2, DH], BF16)
         tables_ch = keep.tile([P, 2, S], BF16)
-        cos_tok, sin_tok = tables_tok[:, 0, :, :], tables_tok[:, 1, :, :]
-        cos_ch, sin_ch = tables_ch[:, 0, :], tables_ch[:, 1, :]
         x_raw = keep.tile([P, TILES, E], BF16)
         x_grouped = keep.tile([P, PASSES, TILES, P, PACK], BF16, align_bytes=64)
         x_codes = keep.tile([P, PASSES, S], U32, align_bytes=64)
         x_scales = keep.tile([P, PASSES, S], U8, align_bytes=64)
-        w_codes = keep.tile([P, 6, PASSES, BLK], U32, align_bytes=64)
-        w_scales = keep.tile([P, 6, PASSES, BLK], U8, align_bytes=64)
+        w_codes = keep.tile([P, BLOCKS, PASSES, BLK], U32, align_bytes=64)
+        w_scales = keep.tile([P, BLOCKS, PASSES, BLK], U8, align_bytes=64)
 
         w_raw, w_grouped, results, products = {}, {}, {}, {}
 
@@ -102,7 +88,7 @@ def tile_arlowvisionattention_pa_kernel(tc, hidden_states, cos, sin, w_qkv, b_qk
             nc.sync.dma_start(out=x_raw[:, tiles, :], in_=x_rows[:, tiles, :])
 
         def interleave_w(copy, blk, g, n0, n1):
-            if n0 == 0 and g == 0:
+            if blk not in w_grouped:
                 w_grouped[blk] = w_grouped_pool.tile([P, PASSES, BLK, PACK], BF16, name="grouped", align_bytes=64)
             copy(
                 out=w_grouped[blk][:, g, n0:n1, :].rearrange("p (c i) t -> p c t i", i=4),
@@ -116,16 +102,14 @@ def tile_arlowvisionattention_pa_kernel(tc, hidden_states, cos, sin, w_qkv, b_qk
                 in_=w_grouped[blk][:, passes, :, :].rearrange("p g n t -> p (g n t)"),
             )
 
-        def turn_x(j, copy):
+        def turn_x(j):
             words = x_raw[:, j, :].bitcast(F32)
             turned = turned_pool.tile([P, PASSES, 2, P], F32, name="turned")
             for g in range(PASSES):
                 for u in range(2):
                     nc.tensor.transpose(turned[:, g, u, :], words[:, 2 * P * g + u : 2 * P * (g + 1) : 2], ident[:])
             dst = x_grouped[:, :, j, :, :].rearrange("p g r t -> p g (r t)").bitcast(F32)
-            copy(
-                out=dst.rearrange("p g (r u) -> p g r u", u=2), in_=turned[:].rearrange("p g u r -> p g r u")
-            )
+            nc.scalar.copy(out=dst.rearrange("p g (r u) -> p g r u", u=2), in_=turned[:].rearrange("p g u r -> p g r u"))
 
         def quantize_x(pair):
             tokens = slice(2 * pair * P, (2 * pair + 2) * P)
@@ -135,6 +119,31 @@ def tile_arlowvisionattention_pa_kernel(tc, hidden_states, cos, sin, w_qkv, b_qk
                     scales=x_scales[:, g, tokens],
                     in_=x_grouped[:, g, 2 * pair : 2 * pair + 2, :, :].rearrange("p j r t -> p (j r t)"),
                 )
+
+        def spread_bias(which):
+            spread = turned_pool.tile([P, W], BF16, name="turned")
+            for r in range(W // P):
+                row = which * (W // P) + r
+                nc.tensor.matmul(
+                    spread[:, r * P : (r + 1) * P],
+                    lhsT=ident_bf[:, row : row + 1].to_broadcast([P, P]),
+                    rhs=bias_rows[:],
+                    start=True,
+                    stop=True,
+                )
+            nc.scalar.copy(out=bias_all[:, which * W : (which + 1) * W], in_=spread[:])
+
+        def turn_table(which):
+            turned = turned_pool.tile([P, S], BF16, name="turned")
+            for j in range(TILES):
+                nc.tensor.matmul(
+                    turned[:, j * P : (j + 1) * P],
+                    lhsT=tables_twice[:, which, j, :, :].rearrange("p r d -> p (r d)"),
+                    rhs=ident_bf[:],
+                    start=True,
+                    stop=True,
+                )
+            nc.scalar.copy(out=tables_ch[:, which, :], in_=turned[:])
 
         def project(dst, blk, channels, tokens, tokens_on_partitions):
             for g in range(PASSES):
@@ -151,11 +160,6 @@ def tile_arlowvisionattention_pa_kernel(tc, hidden_states, cos, sin, w_qkv, b_qk
                     stop=(g == PASSES - 1),
                 )
 
-        def project_token_tile(blk, j):
-            sums = sums_pool.tile([P, BLK], F32, name="sums")
-            project(sums[:], blk, slice(0, BLK), slice(j * P, (j + 1) * P), True)
-            return sums
-
         def result_of(blk):
             if blk not in results:
                 results[blk] = result_pool.tile([P, TILES, BLK], F32, name="result")
@@ -167,54 +171,23 @@ def tile_arlowvisionattention_pa_kernel(tc, hidden_states, cos, sin, w_qkv, b_qk
                 out=outs[blk // 2][:, j0:j1, first_col + c0 : first_col + c1], in_=results[blk][:, j0:j1, c0:c1]
             )
 
-        def value_tile(blk, j, on_gpsimd):
-            sums = project_token_tile(blk, j)
+        def value_unit(blk, j):
+            sums = sums_pool.tile([P, BLK], F32, name="sums")
+            project(sums[:], blk, slice(0, BLK), slice(j * P, (j + 1) * P), True)
             bias = bias_all[:, blk * BLK : (blk + 1) * BLK]
-            if on_gpsimd:
-                plain = work.tile([P, BLK], F32, bufs=2)
-                nc.scalar.copy(out=plain[:], in_=sums[:])
-                nc.gpsimd.tensor_tensor(out=result_of(blk)[:, j, :], in0=plain[:], in1=bias, op=ADD)
-            else:
-                nc.vector.tensor_tensor(out=result_of(blk)[:, j, :], in0=sums[:], in1=bias, op=ADD)
-
-        def spread_bias(which):
-            spread = turned_pool.tile([P, W], BF16, name="turned")
-            for r in range(W // P):
-                row = which * (W // P) + r
-                nc.tensor.matmul(
-                    spread[:, r * P : (r + 1) * P],
-                    lhsT=ident_bf[:, row : row + 1].to_broadcast([P, P]),
-                    rhs=bias_rows[:],
-                    start=True,
-                    stop=True,
-                )
-            nc.scalar.copy(out=bias_all[:, which * W : (which + 1) * W], in_=spread[:])
-
-        def turn_table(twice, table):
-            turned = turned_pool.tile([P, S], BF16, name="turned")
-            for j in range(TILES):
-                nc.tensor.matmul(
-                    turned[:, j * P : (j + 1) * P],
-                    lhsT=twice[:, j, :, :].rearrange("p r d -> p (r d)"),
-                    rhs=ident_bf[:],
-                    start=True,
-                    stop=True,
-                )
-            nc.scalar.copy(out=table, in_=turned[:])
-
-        def turn_and_add(dst, with_cos, with_sin):
-            nc.tensor.matmul(dst, lhsT=with_cos, rhs=ident[:], start=True, stop=False, is_transpose=True)
-            nc.tensor.matmul(dst, lhsT=with_sin, rhs=pair_swap[:], start=False, stop=True, is_transpose=True)
+            nc.vector.tensor_tensor(out=result_of(blk)[:, j, :], in0=sums[:], in1=bias, op=ADD)
+            store(blk, j, j + 1, 0, BLK)
 
         def channel_unit(blk, c, half):
             tokens = slice(half * HALF * P, (half + 1) * HALF * P)
             sums = sums_pool.tile([P, HALF * P], F32, name="sums")
             project(sums[:], blk, slice(c * P, (c + 1) * P), tokens, False)
             product = work.tile([P, 2, HALF * P], F32, bufs=STEP_UNITS * (LAG + 1))
+            row = blk * CH_TILES + c
             nc.vector.scalar_tensor_tensor(
                 out=product[:],
                 in0=sums[:].unsqueeze(1).to_broadcast([P, 2, HALF * P]),
-                scalar=bias_cols[:, blk * CH_TILES + c : blk * CH_TILES + c + 1],
+                scalar=bias_cols[:, row : row + 1],
                 in1=tables_ch[:, :, tokens],
                 op0=ADD,
                 op1=MULT,
@@ -225,49 +198,61 @@ def tile_arlowvisionattention_pa_kernel(tc, hidden_states, cos, sin, w_qkv, b_qk
             product = products.pop((blk, c, half))
             turned = turned_pool.tile([P, HALF, P], F32, name="turned")
             for s in range(HALF):
-                turn_and_add(turned[:, s, :], product[:, 0, s * P : (s + 1) * P], product[:, 1, s * P : (s + 1) * P])
+                tokens = slice(s * P, (s + 1) * P)
+                for which, moving in enumerate((ident, pair_swap)):
+                    nc.tensor.matmul(
+                        turned[:, s, :],
+                        lhsT=product[:, which, tokens],
+                        rhs=moving[:],
+                        start=(which == 0),
+                        stop=(which == 1),
+                        is_transpose=True,
+                    )
             nc.scalar.copy(out=result_of(blk)[:, half * HALF : (half + 1) * HALF, c * P : (c + 1) * P], in_=turned[:])
             if c % 2 == 1:
                 store(blk, half * HALF, (half + 1) * HALF, (c - 1) * P, (c + 1) * P)
 
-        def token_unit(blk, pair, col_half, before_bias):
+        def token_unit(blk, pair):
             j0 = HALF + 2 * pair
-            cols = slice(col_half * BLK // 2, (col_half + 1) * BLK // 2)
-            sums = sums_pool.tile([P, 2, BLK // 2], F32, name="sums")
+            width = BLK // 2
+            cols = slice(width, BLK)
+            sums = sums_pool.tile([P, 2, width], F32, name="sums")
             for i in range(2):
                 project(sums[:, i, :], blk, cols, slice((j0 + i) * P, (j0 + i + 1) * P), True)
-            before_bias()
-            biased = work.tile([P, 2, BLK // 2], F32, bufs=BIASED_BUFS)
-            tok_cos = work.tile([P, 2, BLK // 2], F32, bufs=1)
-            tok_sin = work.tile([P, 2, BLK // 2], F32, bufs=1)
-            bias = bias_all[:, blk * BLK : (blk + 1) * BLK][:, cols]
-            nc.vector.tensor_tensor(
-                out=biased[:], in0=sums[:], in1=bias.unsqueeze(1).to_broadcast([P, 2, BLK // 2]), op=ADD
-            )
-            heads = BLK // 2 // DH
-            for dst, table in ((tok_cos, cos_tok), (tok_sin, sin_tok)):
+            biased = work.tile([P, 2, width], F32, bufs=2)
+            tok_product = work.tile([P, 2, 2, width], F32)
+            bias = bias_all[:, blk * BLK + width : (blk + 1) * BLK]
+            nc.vector.tensor_tensor(out=biased[:], in0=sums[:], in1=bias.unsqueeze(1).to_broadcast([P, 2, width]), op=ADD)
+            for which in range(2):
                 nc.gpsimd.tensor_tensor(
-                    out=dst[:].rearrange("p j (h d) -> p j h d", d=DH),
+                    out=tok_product[:, which, :, :].rearrange("p j (h d) -> p j h d", d=DH),
                     in0=biased[:].rearrange("p j (h d) -> p j h d", d=DH),
-                    in1=table[:, j0 : j0 + 2, :].unsqueeze(2).to_broadcast([P, 2, heads, DH]),
+                    in1=tables_tok[:, which, j0 : j0 + 2, :].unsqueeze(2).to_broadcast([P, 2, width // DH, DH]),
                     op=MULT,
                 )
             nc.gpsimd.tensor_tensor(
                 out=result_of(blk)[:, j0 : j0 + 2, cols].rearrange("p j (n e) -> p j n e", e=2),
-                in0=tok_cos[:].rearrange("p j (n e) -> p j n e", e=2),
-                in1=tok_sin[:].rearrange("p j (n e) -> p j n e", e=2)[:, :, :, ::-1],
+                in0=tok_product[:, 0, :, :].rearrange("p j (n e) -> p j n e", e=2),
+                in1=tok_product[:, 1, :, :].rearrange("p j (n e) -> p j n e", e=2)[:, :, :, ::-1],
                 op=ADD,
             )
 
         nc.vector.memset(bias_rows[:], 0.0)
         bias_src = b_qkv.rearrange("(r c) -> r c", c=P)
-        rot_rows = 2 * W // P
-        if HEAD_ORDER:
-            load_w(W_ORDER[0], 0)
         nc.sync.dma_start(out=sin_raw[:], in_=sin.rearrange("(p j) d -> p j d", j=TILES))
-        nc.sync.dma_start(out=cos_tok, in_=cos.rearrange("(p j) d -> p j d", j=TILES))
-        nc.sync.dma_start(out=bias_rows[0:rot_rows, :], in_=bias_src[0:rot_rows, :])
-        nc.sync.dma_start(out=bias_rows[rot_rows : 3 * W // P, :], in_=bias_src[rot_rows:, :])
+        nc.sync.dma_start(out=tables_tok[:, 0, :, :], in_=cos.rearrange("(p j) d -> p j d", j=TILES))
+        nc.sync.dma_start(out=bias_rows[0:ROT_ROWS, :], in_=bias_src[0:ROT_ROWS, :])
+        nc.sync.dma_start(out=bias_rows[ROT_ROWS:BIAS_ROWS, :], in_=bias_src[ROT_ROWS:, :])
+        first = W_ORDER[0]
+        for g in range(PASSES):
+            load_x(g)
+            load_w(first, g)
+        load_x(2)
+        load_x(3)
+        for blk in W_ORDER[1 : RAW_BUFS // PASSES]:
+            for g in range(PASSES):
+                load_w(blk, g)
+
         make_identity(nc, ident[:])
         nc.vector.memset(signs[:, 0:1], 1.0)
         nc.vector.memset(signs[:, 1:2], -1.0)
@@ -276,25 +261,8 @@ def tile_arlowvisionattention_pa_kernel(tc, hidden_states, cos, sin, w_qkv, b_qk
             out=pair_swap[:].rearrange("p (n e) -> p n e", e=2),
             in_=ident[:].rearrange("p (n e) -> p n e", e=2)[:, :, ::-1],
         )
-
-        first = W_ORDER[0]
-        if not HEAD_ORDER:
-            load_w(first, 0)
-        load_x(0)
-        load_x(1)
-        load_w(first, 1)
-        load_x(2)
-        load_x(3)
-        load_w(W_ORDER[1], 0)
-        load_w(W_ORDER[1], 1)
-        for blk in W_ORDER[2:4]:
-            load_w(blk, 0)
-            load_w(blk, 1)
-
-        if HEAD_ORDER:
-            interleave_w(nc.vector.tensor_copy, first, 0, 0, BLK)
         nc.vector.tensor_tensor(
-            out=sin_tok.rearrange("p j (n e) -> p (j n) e", e=2),
+            out=tables_tok[:, 1, :, :].rearrange("p j (n e) -> p (j n) e", e=2),
             in0=sin_raw[:].rearrange("p j (n e) -> p (j n) e", e=2)[:, :, ::-1],
             in1=signs[:].unsqueeze(1).to_broadcast([P, TILES * DH // 2, 2]),
             op=MULT,
@@ -302,125 +270,109 @@ def tile_arlowvisionattention_pa_kernel(tc, hidden_states, cos, sin, w_qkv, b_qk
         spread_bias(0)
         bias_turned = turned_pool.tile([P, P], BF16, name="turned")
         nc.tensor.transpose(bias_turned[:], bias_rows[:], ident_bf[:])
-        nc.vector.tensor_copy(out=cos_twice[:], in_=cos_tok.unsqueeze(2).to_broadcast([P, TILES, 2, DH]))
-        nc.vector.tensor_copy(out=sin_twice[:], in_=sin_tok.unsqueeze(2).to_broadcast([P, TILES, 2, DH]))
-        nc.scalar.copy(out=bias_cols[:], in_=bias_turned[:, 0 : 2 * W // P])
-        turn_table(cos_twice, cos_ch)
-        if not HEAD_ORDER:
-            interleave_w(nc.vector.tensor_copy, first, 0, 0, BLK)
-        turn_table(sin_twice, sin_ch)
-        turn_x(0, nc.scalar.copy)
-        quantize_w(first, slice(0, 1))
-        turn_x(1, nc.vector.tensor_copy)
+        for which in range(2):
+            nc.vector.tensor_copy(
+                out=tables_twice[:, which, :, :, :],
+                in_=tables_tok[:, which, :, :].unsqueeze(2).to_broadcast([P, TILES, 2, DH]),
+            )
+        nc.scalar.copy(out=bias_cols[:], in_=bias_turned[:, 0:ROT_ROWS])
+
+        for g in range(PASSES):
+            turn_x(2 * g)
+            turn_x(2 * g + 1)
+            if g > 0:
+                quantize_w(first, slice(g - 1, g))
+            turn_table(g)
+            interleave_w(nc.vector.tensor_copy, first, g, 0, BLK)
+            quantize_x(g)
         spread_bias(2)
-        turn_x(2, nc.scalar.copy)
-        turn_x(3, nc.scalar.copy)
-        quantize_x(0)
-        interleave_w(nc.vector.tensor_copy, first, 1, 0, HEAD_SPLIT)
-        interleave_w(nc.scalar.copy, first, 1, HEAD_SPLIT, BLK)
-        spread_bias(1)
-        quantize_x(1)
-        quantize_w(first, slice(1, 2))
-        for blk in W_ORDER[4:]:
-            load_w(blk, 0)
-            load_w(blk, 1)
-        turn_x(4, nc.scalar.copy)
-        turn_x(5, nc.scalar.copy)
+        quantize_w(first, slice(PASSES - 1, PASSES))
+        for blk in W_ORDER[RAW_BUFS // PASSES :]:
+            for g in range(PASSES):
+                load_w(blk, g)
+        turn_x(4)
+        turn_x(5)
 
-        halves = [(blk, g) for blk in W_ORDER[1:] for g in range(PASSES)]
-        pieces = [(blk, g, n0) for blk, g in halves for n0 in range(0, BLK, PIECE)]
+        pieces = [(blk, g, n0) for blk in W_ORDER[1:] for g in range(PASSES) for n0 in range(0, BLK, PIECE)]
         grouped_at = []
+        quantised_at = {}
 
-        def next_pieces(count, step):
+        def take_pieces(copy, count, step):
+            blk, g, n0 = pieces[0]
+            count = min(count, (BLK - n0) // PIECE)
+            for i in range(count):
+                pieces.pop(0)
+            interleave_w(copy, blk, g, n0, n0 + count * PIECE)
+            if n0 + count * PIECE == BLK and g == PASSES - 1:
+                grouped_at.append((step, blk))
+
+        def scalar_pieces(count, step):
             for i in range(min(count, len(pieces))):
-                blk, g, n0 = pieces.pop(0)
-                interleave_w(nc.scalar.copy, blk, g, n0, n0 + PIECE)
-                if n0 + PIECE == BLK and g == PASSES - 1:
-                    grouped_at.append((step, blk, slice(0, PASSES)))
+                take_pieces(nc.scalar.copy, 1, step)
 
-        def vector_pieces(step):
-            if pieces and V_TAKE[0] <= step < V_TAKE[1]:
-                blk, g, n0 = pieces[0]
-                count = min(V_TAKE[2], (BLK - n0) // PIECE)
-                del_count = [pieces.pop(0) for i in range(count)]
-                interleave_w(nc.vector.tensor_copy, blk, g, n0, n0 + count * PIECE)
-                if n0 + count * PIECE == BLK and g == PASSES - 1:
-                    grouped_at.append((step, blk, slice(0, PASSES)))
+        def finish_step(units, step):
+            channel_units = [unit[1:] for unit in units if unit[0] == "channel"]
+            scalar_pieces(PIECES_PER_STEP - len(channel_units), step)
+            for unit in channel_units:
+                finish_channel_unit(*unit)
+                scalar_pieces(1, step)
 
-        def quantize_grouped(step):
-            if grouped_at and grouped_at[0][0] + Q_DELAY <= step:
-                quantize_w(*grouped_at.pop(0)[1:])
-
-        def block_units(blk, n_token):
-            first_half = [("ch", blk, c, 0) for c in range(CH_TILES)]
-            second_half = [("ch", blk, c, 1) for c in range(CH_TILES - n_token)]
-            by_token = [("tok", blk, pair, 1 - i) for i in range(n_token // 2) for pair in range(2)]
-            if n_token == 2:
-                second_half = [by_token[0], second_half[0], by_token[1], second_half[1]]
-            elif n_token == 4:
-                second_half = by_token
-            return first_half[:2] + [second_half[0], first_half[2], second_half[1], first_half[3]] + second_half[2:]
-
-        units = [u for blk, n in zip(ROT_BLOCKS, TOKEN_UNITS) for u in block_units(blk, n)]
+        units = []
+        for blk in ROT_BLOCKS:
+            second_half = [("token", blk, 0), ("channel", blk, 0, 1), ("token", blk, 1), ("channel", blk, 1, 1)]
+            units += [("channel", blk, 0, 0), ("channel", blk, 1, 0), second_half[0], ("channel", blk, 2, 0)]
+            units += [second_half[1], ("channel", blk, 3, 0), second_half[2], second_half[3]]
         steps = [units[i : i + STEP_UNITS] for i in range(0, len(units), STEP_UNITS)]
-        pending_stores = []
-
-        def value_unit(blk, j, step):
-            on_gpsimd = GP_STEPS[0] <= step < GP_STEPS[1] and j % GP_SHARE == 0
-            value_tile(blk, j, on_gpsimd)
-            if on_gpsimd:
-                pending_stores.append((step, blk, j, j + 1, 0, BLK))
-            else:
-                store(blk, j, j + 1, 0, BLK)
-
-        def finish_step(step, now):
-            done = [u for u in steps[step] if u[0] == "ch"]
-            next_pieces(PIECES[now % 2] - len(done), now)
-            for kind, blk, a, b in done:
-                finish_channel_unit(blk, a, b)
-                next_pieces(1, now)
 
         first_values = list(range(TILES))
         last_values = list(range(TILES))
-        for step in range(len(steps)):
-            for kind, blk, a, b in steps[step]:
-                if kind == "ch":
-                    channel_unit(blk, a, b)
+        token_stores = []
+        for step, step_units in enumerate(steps):
+            late_stores = list(token_stores)
+            token_stores.clear()
+            for unit in step_units:
+                if unit[0] == "channel":
+                    channel_unit(*unit[1:])
                 else:
-                    token_unit(blk, a, b, lambda: quantize_grouped(step) if Q_BEFORE else None)
-                    pending_stores.append((step, blk, HALF + 2 * a, HALF + 2 * a + 2, b * BLK // 2, (b + 1) * BLK // 2))
-                if (kind, blk, a, b) == units[0]:
+                    blk, pair = unit[1:]
+                    token_unit(blk, pair)
+                    token_stores.append((blk, HALF + 2 * pair, HALF + 2 * pair + 2, BLK // 2, BLK))
+                if unit == units[0]:
                     quantize_x(2)
-                if (kind, blk, a, b) == units[1]:
-                    turn_x(6, nc.scalar.copy)
-                    turn_x(7, nc.scalar.copy)
-                if (kind, blk, a, b) == units[2]:
+                if unit == units[1]:
+                    scalar_pieces(PIECES_PER_STEP // 2, step)
+                    turn_x(6)
+                    turn_x(7)
+                    spread_bias(1)
+                    scalar_pieces(PIECES_PER_STEP // 2, step)
+                if unit == units[2]:
                     quantize_x(3)
-                if kind == "tok":
-                    if not Q_BEFORE:
-                        quantize_grouped(step)
-                    vector_pieces(step)
-            if step == 0:
-                next_pieces(EARLY[1], step)
-            if step == 1:
-                next_pieces(EARLY[2], step)
-            if step >= V_START[0]:
-                for j in first_values[:V_FIRST]:
-                    value_unit(V_BLOCKS[0], first_values.pop(0), step)
-            if step >= V_START[1]:
-                for j in last_values[:V_LAST]:
-                    value_unit(V_BLOCKS[1], last_values.pop(0), step)
+                if unit[0] == "token":
+                    if grouped_at and grouped_at[0][0] < step:
+                        ready = grouped_at.pop(0)[1]
+                        quantize_w(ready, slice(0, PASSES))
+                        quantised_at[ready] = step
+                    if step in HELP_STEPS:
+                        take_pieces(nc.vector.tensor_copy, HELP_PIECES, step)
+            values = []
+            if quantised_at.get(V_FIRST, step) < step:
+                values += [(V_FIRST, first_values.pop(0)) for j in first_values[:VALUES_PER_STEP]]
+            if step >= len(steps) - LAG:
+                values += [(V_LAST, last_values.pop(0)) for j in last_values[:VALUES_PER_STEP]]
+            for blk, j in values:
+                value_unit(blk, j)
             if step >= LAG:
-                finish_step(step - LAG, step)
-            for entry in [e for e in pending_stores if e[0] + STORE_LAG <= step]:
-                pending_stores.remove(entry)
-                store(*entry[1:])
-        for j in last_values[:TAIL_FIRST]:
-            value_unit(V_BLOCKS[1], j, len(steps))
-        for step in range(len(steps) - LAG, len(steps)):
-            finish_step(step, len(steps))
-        for j in last_values[TAIL_FIRST:-1]:
-            value_unit(V_BLOCKS[1], j, len(steps))
-        for args in pending_stores:
-            store(*args[1:])
-        value_unit(V_BLOCKS[1], last_values[-1], len(steps))
+                finish_step(steps[step - LAG], step)
+            elif step > 0:
+                scalar_pieces(PIECES_PER_STEP, step)
+            for args in late_stores:
+                store(*args)
+
+        value_unit(V_LAST, last_values[0])
+        for step_units in steps[len(steps) - LAG :]:
+            finish_step(step_units, len(steps))
+        for j in last_values[1:-1]:
+            value_unit(V_LAST, j)
+        for args in token_stores:
+            store(*args)
+        value_unit(V_LAST, last_values[-1])

@@ -36,7 +36,7 @@ LAG = 2
 SUMS_BANKS = 5
 PIECE = 128
 PIECES_PER_STEP = 4
-HELP_STEPS = (3, 5)
+HELP_STEP = 3
 HELP_PIECES = 2
 VALUES_PER_STEP = 2
 RAW_BUFS = 8
@@ -67,6 +67,7 @@ def tile_arlowvisionattention_pa_kernel(tc, hidden_states, cos, sin, w_qkv, b_qk
         sin_raw = keep.tile([P, TILES, DH], BF16)
         tables_tok = keep.tile([P, 2, TILES, DH], BF16)
         tables_twice = keep.tile([P, 2, TILES, 2, DH], BF16)
+        tables_heads = keep.tile([P, 2, HALF, BLK // 2 // DH, DH], F32)
         tables_ch = keep.tile([P, 2, S], BF16)
         x_raw = keep.tile([P, TILES, E], BF16)
         x_grouped = keep.tile([P, PASSES, TILES, P, PACK], BF16, align_bytes=64)
@@ -223,13 +224,12 @@ def tile_arlowvisionattention_pa_kernel(tc, hidden_states, cos, sin, w_qkv, b_qk
             tok_product = work.tile([P, 2, 2, width], F32)
             bias = bias_all[:, blk * BLK + width : (blk + 1) * BLK]
             nc.vector.tensor_tensor(out=biased[:], in0=sums[:], in1=bias.unsqueeze(1).to_broadcast([P, 2, width]), op=ADD)
-            for which in range(2):
-                nc.gpsimd.tensor_tensor(
-                    out=tok_product[:, which, :, :].rearrange("p j (h d) -> p j h d", d=DH),
-                    in0=biased[:].rearrange("p j (h d) -> p j h d", d=DH),
-                    in1=tables_tok[:, which, j0 : j0 + 2, :].unsqueeze(2).to_broadcast([P, 2, width // DH, DH]),
-                    op=MULT,
-                )
+            nc.gpsimd.tensor_tensor(
+                out=tok_product[:].rearrange("p m j n -> p m (j n)"),
+                in0=biased[:].rearrange("p j n -> p (j n)").unsqueeze(1).to_broadcast([P, 2, 2 * width]),
+                in1=tables_heads[:, :, 2 * pair : 2 * pair + 2, :, :].rearrange("p m j h d -> p m (j h d)"),
+                op=MULT,
+            )
             nc.gpsimd.tensor_tensor(
                 out=result_of(blk)[:, j0 : j0 + 2, cols].rearrange("p j (n e) -> p j n e", e=2),
                 in0=tok_product[:, 0, :, :].rearrange("p j (n e) -> p j n e", e=2),
@@ -274,6 +274,11 @@ def tile_arlowvisionattention_pa_kernel(tc, hidden_states, cos, sin, w_qkv, b_qk
             nc.vector.tensor_copy(
                 out=tables_twice[:, which, :, :, :],
                 in_=tables_tok[:, which, :, :].unsqueeze(2).to_broadcast([P, TILES, 2, DH]),
+            )
+        for which in range(2):
+            nc.vector.tensor_copy(
+                out=tables_heads[:, which, :, :, :],
+                in_=tables_tok[:, which, HALF:, :].unsqueeze(2).to_broadcast([P, HALF, BLK // 2 // DH, DH]),
             )
         nc.scalar.copy(out=bias_cols[:], in_=bias_turned[:, 0:ROT_ROWS])
 
@@ -352,7 +357,7 @@ def tile_arlowvisionattention_pa_kernel(tc, hidden_states, cos, sin, w_qkv, b_qk
                         ready = grouped_at.pop(0)[1]
                         quantize_w(ready, slice(0, PASSES))
                         quantised_at[ready] = step
-                    if step in HELP_STEPS:
+                    if step == HELP_STEP:
                         take_pieces(nc.vector.tensor_copy, HELP_PIECES, step)
             values = []
             if quantised_at.get(V_FIRST, step) < step:

from contextlib import ExitStack

import concourse.mybir as mybir
from concourse.masks import make_identity

S, E, H, DH = 1024, 1024, 16, 64
W = H * DH
FLOPS = 2 * S * E * 3 * W

F32 = mybir.dt.float32
BF16 = mybir.dt.bfloat16
U32 = mybir.dt.uint32
U8 = mybir.dt.uint8
FP8X4 = mybir.dt.float8_e5m2_x4
ADD = mybir.AluOpType.add
MULT = mybir.AluOpType.mult

P = 128
PACK = 4
K_PASS = P * PACK
PASSES = E // K_PASS
TILES = S // P
HALF = TILES // 2
BLK = 512
BLOCKS = 3 * W // BLK
CH_TILES = BLK // P
BIAS_ROWS = 3 * W // P
ROT_ROWS = 2 * W // P

ROT_BLOCKS = (0, 1, 2, 3)
V_FIRST, V_LAST = 4, 5
W_ORDER = (0, 1, V_FIRST, 2, 3, V_LAST)

STEP_UNITS = 2
LAG = 2
SUMS_BANKS = 5
PIECE = 128
PIECES_PER_STEP = 4
HELP_STEP = 3
HELP_PIECES = 2
VALUES_PER_STEP = 2
RAW_BUFS = 8


def tile_arlowvisionattention_pa_kernel(tc, hidden_states, cos, sin, w_qkv, b_qkv, out_0, out_1, out_2):
    nc = tc.nc
    outs = [o.rearrange("(p j) h d -> p j (h d)", j=TILES) for o in (out_0, out_1, out_2)]
    x_rows = hidden_states.rearrange("(p j) k -> p j k", j=TILES)

    with ExitStack() as ctx:
        keep = ctx.enter_context(tc.tile_pool(name="keep", bufs=1))
        w_raw_pool = ctx.enter_context(tc.tile_pool(name="w_raw", bufs=RAW_BUFS))
        w_grouped_pool = ctx.enter_context(tc.tile_pool(name="w_grouped", bufs=2))
        work = ctx.enter_context(tc.tile_pool(name="work", bufs=1))
        result_pool = ctx.enter_context(tc.tile_pool(name="result", bufs=3))
        sums_pool = ctx.enter_context(tc.psum_pool(name="sums", bufs=SUMS_BANKS))
        turned_pool = ctx.enter_context(tc.psum_pool(name="turned", bufs=8 - SUMS_BANKS))
        ctx.enter_context(tc.manual_schedule())

        ident = keep.tile([P, P], F32)
        ident_bf = keep.tile([P, P], BF16)
        pair_swap = keep.tile([P, P], F32)
        signs = keep.tile([P, 2], BF16)
        bias_rows = keep.tile([P, P], BF16)
        bias_cols = keep.tile([P, ROT_ROWS], F32)
        bias_all = keep.tile([P, 3 * W], BF16)
        sin_raw = keep.tile([P, TILES, DH], BF16)
        tables_tok = keep.tile([P, 2, TILES, DH], BF16)
        tables_twice = keep.tile([P, 2, TILES, 2, DH], BF16)
        tables_heads = keep.tile([P, 2, HALF, BLK // 2 // DH, DH], F32)
        tables_ch = keep.tile([P, 2, S], BF16)
        x_raw = keep.tile([P, TILES, E], BF16)
        x_grouped = keep.tile([P, PASSES, TILES, P, PACK], BF16, align_bytes=64)
        x_codes = keep.tile([P, PASSES, S], U32, align_bytes=64)
        x_scales = keep.tile([P, PASSES, S], U8, align_bytes=64)
        w_codes = keep.tile([P, BLOCKS, PASSES, BLK], U32, align_bytes=64)
        w_scales = keep.tile([P, BLOCKS, PASSES, BLK], U8, align_bytes=64)

        w_raw, w_grouped, results, products = {}, {}, {}, {}

        def load_w(blk, g):
            raw = w_raw_pool.tile([P, PACK, BLK], BF16, name="raw")
            rows = w_qkv[g * K_PASS : (g + 1) * K_PASS, blk * BLK : (blk + 1) * BLK]
            nc.sync.dma_start(out=raw[:], in_=rows.rearrange("(p t) n -> p t n", t=PACK))
            w_raw[blk, g] = raw

        def load_x(pair):
            tiles = slice(2 * pair, 2 * pair + 2)
            nc.sync.dma_start(out=x_raw[:, tiles, :], in_=x_rows[:, tiles, :])

        def interleave_w(copy, blk, g, n0, n1):
            if blk not in w_grouped:
                w_grouped[blk] = w_grouped_pool.tile([P, PASSES, BLK, PACK], BF16, name="grouped", align_bytes=64)
            copy(
                out=w_grouped[blk][:, g, n0:n1, :].rearrange("p (c i) t -> p c t i", i=4),
                in_=w_raw[blk, g][:, :, n0:n1].rearrange("p t (c i) -> p c t i", i=4),
            )

        def quantize_w(blk, passes):
            nc.vector.quantize_mx(
                out=w_codes[:, blk, passes, :].rearrange("p g n -> p (g n)").bitcast(FP8X4),
                scales=w_scales[:, blk, passes, :].rearrange("p g n -> p (g n)"),
                in_=w_grouped[blk][:, passes, :, :].rearrange("p g n t -> p (g n t)"),
            )

        def turn_x(j):
            words = x_raw[:, j, :].bitcast(F32)
            turned = turned_pool.tile([P, PASSES, 2, P], F32, name="turned")
            for g in range(PASSES):
                for u in range(2):
                    nc.tensor.transpose(turned[:, g, u, :], words[:, 2 * P * g + u : 2 * P * (g + 1) : 2], ident[:])
            dst = x_grouped[:, :, j, :, :].rearrange("p g r t -> p g (r t)").bitcast(F32)
            nc.scalar.copy(out=dst.rearrange("p g (r u) -> p g r u", u=2), in_=turned[:].rearrange("p g u r -> p g r u"))

        def quantize_x(pair):
            tokens = slice(2 * pair * P, (2 * pair + 2) * P)
            for g in range(PASSES):
                nc.vector.quantize_mx(
                    out=x_codes[:, g, tokens].bitcast(FP8X4),
                    scales=x_scales[:, g, tokens],
                    in_=x_grouped[:, g, 2 * pair : 2 * pair + 2, :, :].rearrange("p j r t -> p (j r t)"),
                )

        def spread_bias(which):
            spread = turned_pool.tile([P, W], BF16, name="turned")
            for r in range(W // P):
                row = which * (W // P) + r
                nc.tensor.matmul(
                    spread[:, r * P : (r + 1) * P],
                    lhsT=ident_bf[:, row : row + 1].to_broadcast([P, P]),
                    rhs=bias_rows[:],
                    start=True,
                    stop=True,
                )
            nc.scalar.copy(out=bias_all[:, which * W : (which + 1) * W], in_=spread[:])

        def turn_table(which):
            turned = turned_pool.tile([P, S], BF16, name="turned")
            for j in range(TILES):
                nc.tensor.matmul(
                    turned[:, j * P : (j + 1) * P],
                    lhsT=tables_twice[:, which, j, :, :].rearrange("p r d -> p (r d)"),
                    rhs=ident_bf[:],
                    start=True,
                    stop=True,
                )
            nc.scalar.copy(out=tables_ch[:, which, :], in_=turned[:])

        def project(dst, blk, channels, tokens, tokens_on_partitions):
            for g in range(PASSES):
                w_side = (w_codes[:, blk, g, channels].bitcast(FP8X4), w_scales[:, blk, g, channels])
                x_side = (x_codes[:, g, tokens].bitcast(FP8X4), x_scales[:, g, tokens])
                fixed, moving = (x_side, w_side) if tokens_on_partitions else (w_side, x_side)
                nc.tensor.matmul_mx(
                    out=dst,
                    lhsT=fixed[0],
                    lhsT_scale=fixed[1],
                    rhs=moving[0],
                    rhs_scale=moving[1],
                    start=(g == 0),
                    stop=(g == PASSES - 1),
                )

        def result_of(blk):
            if blk not in results:
                results[blk] = result_pool.tile([P, TILES, BLK], F32, name="result")
            return results[blk]

        def store(blk, j0, j1, c0, c1):
            first_col = (blk % 2) * BLK
            nc.sync.dma_start(
                out=outs[blk // 2][:, j0:j1, first_col + c0 : first_col + c1], in_=results[blk][:, j0:j1, c0:c1]
            )

        def value_unit(blk, j):
            sums = sums_pool.tile([P, BLK], F32, name="sums")
            project(sums[:], blk, slice(0, BLK), slice(j * P, (j + 1) * P), True)
            bias = bias_all[:, blk * BLK : (blk + 1) * BLK]
            nc.vector.tensor_tensor(out=result_of(blk)[:, j, :], in0=sums[:], in1=bias, op=ADD)
            store(blk, j, j + 1, 0, BLK)

        def channel_unit(blk, c, half):
            tokens = slice(half * HALF * P, (half + 1) * HALF * P)
            sums = sums_pool.tile([P, HALF * P], F32, name="sums")
            project(sums[:], blk, slice(c * P, (c + 1) * P), tokens, False)
            product = work.tile([P, 2, HALF * P], F32, bufs=STEP_UNITS * (LAG + 1))
            row = blk * CH_TILES + c
            nc.vector.scalar_tensor_tensor(
                out=product[:],
                in0=sums[:].unsqueeze(1).to_broadcast([P, 2, HALF * P]),
                scalar=bias_cols[:, row : row + 1],
                in1=tables_ch[:, :, tokens],
                op0=ADD,
                op1=MULT,
            )
            products[blk, c, half] = product

        def finish_channel_unit(blk, c, half):
            product = products.pop((blk, c, half))
            turned = turned_pool.tile([P, HALF, P], F32, name="turned")
            for s in range(HALF):
                tokens = slice(s * P, (s + 1) * P)
                for which, moving in enumerate((ident, pair_swap)):
                    nc.tensor.matmul(
                        turned[:, s, :],
                        lhsT=product[:, which, tokens],
                        rhs=moving[:],
                        start=(which == 0),
                        stop=(which == 1),
                        is_transpose=True,
                    )
            nc.scalar.copy(out=result_of(blk)[:, half * HALF : (half + 1) * HALF, c * P : (c + 1) * P], in_=turned[:])
            if c % 2 == 1:
                store(blk, half * HALF, (half + 1) * HALF, (c - 1) * P, (c + 1) * P)

        def token_unit(blk, pair):
            j0 = HALF + 2 * pair
            width = BLK // 2
            cols = slice(width, BLK)
            sums = sums_pool.tile([P, 2, width], F32, name="sums")
            for i in range(2):
                project(sums[:, i, :], blk, cols, slice((j0 + i) * P, (j0 + i + 1) * P), True)
            biased = work.tile([P, 2, width], F32, bufs=2)
            tok_product = work.tile([P, 2, 2, width], F32)
            bias = bias_all[:, blk * BLK + width : (blk + 1) * BLK]
            nc.vector.tensor_tensor(out=biased[:], in0=sums[:], in1=bias.unsqueeze(1).to_broadcast([P, 2, width]), op=ADD)
            nc.gpsimd.tensor_tensor(
                out=tok_product[:].rearrange("p m j n -> p m (j n)"),
                in0=biased[:].rearrange("p j n -> p (j n)").unsqueeze(1).to_broadcast([P, 2, 2 * width]),
                in1=tables_heads[:, :, 2 * pair : 2 * pair + 2, :, :].rearrange("p m j h d -> p m (j h d)"),
                op=MULT,
            )
            nc.gpsimd.tensor_tensor(
                out=result_of(blk)[:, j0 : j0 + 2, cols].rearrange("p j (n e) -> p j n e", e=2),
                in0=tok_product[:, 0, :, :].rearrange("p j (n e) -> p j n e", e=2),
                in1=tok_product[:, 1, :, :].rearrange("p j (n e) -> p j n e", e=2)[:, :, :, ::-1],
                op=ADD,
            )

        nc.vector.memset(bias_rows[:], 0.0)
        bias_src = b_qkv.rearrange("(r c) -> r c", c=P)
        nc.sync.dma_start(out=sin_raw[:], in_=sin.rearrange("(p j) d -> p j d", j=TILES))
        nc.sync.dma_start(out=tables_tok[:, 0, :, :], in_=cos.rearrange("(p j) d -> p j d", j=TILES))
        nc.sync.dma_start(out=bias_rows[0:ROT_ROWS, :], in_=bias_src[0:ROT_ROWS, :])
        nc.sync.dma_start(out=bias_rows[ROT_ROWS:BIAS_ROWS, :], in_=bias_src[ROT_ROWS:, :])
        first = W_ORDER[0]
        for g in range(PASSES):
            load_x(g)
            load_w(first, g)
        load_x(2)
        load_x(3)
        for blk in W_ORDER[1 : RAW_BUFS // PASSES]:
            for g in range(PASSES):
                load_w(blk, g)

        make_identity(nc, ident[:])
        nc.vector.memset(signs[:, 0:1], 1.0)
        nc.vector.memset(signs[:, 1:2], -1.0)
        nc.vector.tensor_copy(out=ident_bf[:], in_=ident[:])
        nc.vector.tensor_copy(
            out=pair_swap[:].rearrange("p (n e) -> p n e", e=2),
            in_=ident[:].rearrange("p (n e) -> p n e", e=2)[:, :, ::-1],
        )
        nc.vector.tensor_tensor(
            out=tables_tok[:, 1, :, :].rearrange("p j (n e) -> p (j n) e", e=2),
            in0=sin_raw[:].rearrange("p j (n e) -> p (j n) e", e=2)[:, :, ::-1],
            in1=signs[:].unsqueeze(1).to_broadcast([P, TILES * DH // 2, 2]),
            op=MULT,
        )
        spread_bias(0)
        bias_turned = turned_pool.tile([P, P], BF16, name="turned")
        nc.tensor.transpose(bias_turned[:], bias_rows[:], ident_bf[:])
        for which in range(2):
            nc.vector.tensor_copy(
                out=tables_twice[:, which, :, :, :],
                in_=tables_tok[:, which, :, :].unsqueeze(2).to_broadcast([P, TILES, 2, DH]),
            )
        for which in range(2):
            nc.vector.tensor_copy(
                out=tables_heads[:, which, :, :, :],
                in_=tables_tok[:, which, HALF:, :].unsqueeze(2).to_broadcast([P, HALF, BLK // 2 // DH, DH]),
            )
        nc.scalar.copy(out=bias_cols[:], in_=bias_turned[:, 0:ROT_ROWS])

        for g in range(PASSES):
            turn_x(2 * g)
            turn_x(2 * g + 1)
            if g > 0:
                quantize_w(first, slice(g - 1, g))
            turn_table(g)
            interleave_w(nc.vector.tensor_copy, first, g, 0, BLK)
            quantize_x(g)
        spread_bias(2)
        quantize_w(first, slice(PASSES - 1, PASSES))
        for blk in W_ORDER[RAW_BUFS // PASSES :]:
            for g in range(PASSES):
                load_w(blk, g)
        turn_x(4)
        turn_x(5)

        pieces = [(blk, g, n0) for blk in W_ORDER[1:] for g in range(PASSES) for n0 in range(0, BLK, PIECE)]
        grouped_at = []
        quantised_at = {}

        def take_pieces(copy, count, step):
            blk, g, n0 = pieces[0]
            count = min(count, (BLK - n0) // PIECE)
            for i in range(count):
                pieces.pop(0)
            interleave_w(copy, blk, g, n0, n0 + count * PIECE)
            if n0 + count * PIECE == BLK and g == PASSES - 1:
                grouped_at.append((step, blk))

        def scalar_pieces(count, step):
            for i in range(min(count, len(pieces))):
                take_pieces(nc.scalar.copy, 1, step)

        def finish_step(units, step):
            channel_units = [unit[1:] for unit in units if unit[0] == "channel"]
            scalar_pieces(PIECES_PER_STEP - len(channel_units), step)
            for unit in channel_units:
                finish_channel_unit(*unit)
                scalar_pieces(1, step)

        units = []
        for blk in ROT_BLOCKS:
            second_half = [("token", blk, 0), ("channel", blk, 0, 1), ("token", blk, 1), ("channel", blk, 1, 1)]
            units += [("channel", blk, 0, 0), ("channel", blk, 1, 0), second_half[0], ("channel", blk, 2, 0)]
            units += [second_half[1], ("channel", blk, 3, 0), second_half[2], second_half[3]]
        steps = [units[i : i + STEP_UNITS] for i in range(0, len(units), STEP_UNITS)]

        first_values = list(range(TILES))
        last_values = list(range(TILES))
        token_stores = []
        for step, step_units in enumerate(steps):
            late_stores = list(token_stores)
            token_stores.clear()
            for unit in step_units:
                if unit[0] == "channel":
                    channel_unit(*unit[1:])
                else:
                    blk, pair = unit[1:]
                    token_unit(blk, pair)
                    token_stores.append((blk, HALF + 2 * pair, HALF + 2 * pair + 2, BLK // 2, BLK))
                if unit == units[0]:
                    quantize_x(2)
                if unit == units[1]:
                    scalar_pieces(PIECES_PER_STEP // 2, step)
                    turn_x(6)
                    turn_x(7)
                    spread_bias(1)
                    scalar_pieces(PIECES_PER_STEP // 2, step)
                if unit == units[2]:
                    quantize_x(3)
                if unit[0] == "token":
                    if grouped_at and grouped_at[0][0] < step:
                        ready = grouped_at.pop(0)[1]
                        quantize_w(ready, slice(0, PASSES))
                        quantised_at[ready] = step
                    if step == HELP_STEP:
                        take_pieces(nc.vector.tensor_copy, HELP_PIECES, step)
            values = []
            if quantised_at.get(V_FIRST, step) < step:
                values += [(V_FIRST, first_values.pop(0)) for j in first_values[:VALUES_PER_STEP]]
            if step >= len(steps) - LAG:
                values += [(V_LAST, last_values.pop(0)) for j in last_values[:VALUES_PER_STEP]]
            for blk, j in values:
                value_unit(blk, j)
            if step >= LAG:
                finish_step(steps[step - LAG], step)
            elif step > 0:
                scalar_pieces(PIECES_PER_STEP, step)
            for args in late_stores:
                store(*args)

        value_unit(V_LAST, last_values[0])
        for step_units in steps[len(steps) - LAG :]:
            finish_step(step_units, len(steps))
        for j in last_values[1:-1]:
            value_unit(V_LAST, j)
        for args in token_stores:
            store(*args)
        value_unit(V_LAST, last_values[-1])
